import numpy as np
import ml_dtypes


def mxq(x, axis, fmt="e4m3"):
    dtype, down = {"e4m3": (ml_dtypes.float8_e4m3fn, 7), "e5m2": (ml_dtypes.float8_e5m2, 14)}[fmt]
    v = np.moveaxis(np.asarray(x, np.float32).astype(ml_dtypes.bfloat16).astype(np.float64), axis, -1)
    blocks = v.reshape(v.shape[:-1] + (-1, 32))
    amax = np.abs(blocks).max(-1, keepdims=True)
    byte = np.maximum(np.where(amax > 0, np.frexp(amax)[1] - 1 + 127, 0) - down, 1)
    scale = np.exp2(byte - 127.0)
    codes = (blocks / scale).astype(np.float32).astype(dtype).astype(np.float64)
    return np.moveaxis((codes * scale).reshape(v.shape), -1, axis)


WIDE = False


def mx_kscale(k):
    if not WIDE:
        return np.ones(k)
    levels = np.array([10, -10, 5, -5, 0])
    a = np.random.permutation(np.resize(levels, k // 512 * 4)).reshape(k // 512, 4)
    idx = np.arange(k)
    return np.exp2(a[idx // 512, idx % 128 // 32])


BF16 = ml_dtypes.bfloat16


def bf(x):
    return np.asarray(x, np.float32).astype(BF16)


def f64(x):
    return np.asarray(x).astype(np.float64)


E2M1 = np.array([0.0, 0.5, 1.0, 1.5, 2.0, 3.0, 4.0, 6.0, -0.0, -0.5, -1.0, -1.5, -2.0, -3.0, -4.0, -6.0])


def pack_weight(w, fmt):
    k, n = w.shape
    w = f64(bf(w)).reshape(k // 32, 32, n)
    amax = np.abs(w).max(1)
    if fmt == "e4m3":
        byte = np.frexp(amax)[1] - 1 + 127 - 7
    else:
        mant, ex = np.frexp(amax / 6.0)
        byte = np.where(mant > 0.5, ex, ex - 1) + 127
    byte = np.clip(np.where(amax > 0, byte, 1), 1, 254)
    scaled = (w * np.exp2(127.0 - byte)[:, None, :]).reshape(k, n).astype(np.float32)
    by_word = np.ascontiguousarray(scaled.reshape(k // 512, 128, 4, n).transpose(0, 1, 3, 2))
    if fmt == "e4m3":
        words = by_word.astype(ml_dtypes.float8_e4m3fn).view(np.uint8)
    else:
        c = by_word.astype(ml_dtypes.float4_e2m1fn).view(np.uint8) & 0xF
        words = c[..., 0::2] | (c[..., 1::2] << 4)
    return np.ascontiguousarray(words), np.ascontiguousarray(byte.astype(np.uint8).reshape(k // 512, 16, n))


def unpack_weight(words, scales, fmt):
    g, p, n, _ = words.shape
    if fmt == "e4m3":
        vals = np.ascontiguousarray(words).view(ml_dtypes.float8_e4m3fn).astype(np.float64)
    else:
        nib = np.empty((g, p, n, 4), np.uint8)
        nib[..., 0::2] = words & 0xF
        nib[..., 1::2] = words >> 4
        vals = E2M1[nib]
    vals = vals * np.repeat(np.exp2(scales.astype(np.float64) - 127.0), 8, axis=1)[..., None]
    return vals.transpose(0, 1, 3, 2).reshape(g * 512, n)


T, B, D_IN, D_H, D_K, D_OUT = 8, 256, 512, 1024, 1024, 256


def setup_inputs():
    s, t = mx_kscale(D_H), mx_kscale(D_K)
    h1 = bf(np.maximum(np.random.standard_normal((T, B, D_H)), 0.0) * s)
    W2 = np.random.standard_normal((T, D_H, D_K)) * 1.4 / np.sqrt(D_H) / s[:, None] * t
    W2_words, W2_scales = pack_weight(W2.reshape(-1, D_K), "e4m3")
    b2 = bf(np.random.standard_normal((T, D_K)) * 0.2 * t)
    W3 = np.random.standard_normal((T, D_K, D_OUT)) * 1.4 / np.sqrt(D_K) / t[:, None]
    W3_words, W3_scales = pack_weight(W3.reshape(-1, D_OUT), "e4m3")
    b3 = bf(np.random.standard_normal((T, D_OUT)) * 0.2)
    return {"h1": h1,
            "W2_words": W2_words,
            "W2_scales": W2_scales,
            "b2": b2,
            "W3_words": W3_words,
            "W3_scales": W3_scales,
            "b3": b3}


def reference(h1, W2_words, W2_scales, b2, W3_words, W3_scales, b3):
    h2 = np.maximum((mxq(f64(h1), 2, "e4m3") @ unpack_weight(W2_words, W2_scales, "e4m3").reshape(T, D_H, D_K)) + f64(b2)[:, None, :], 0.0)
    out = (mxq(h2, 2, "e4m3") @ unpack_weight(W3_words, W3_scales, "e4m3").reshape(T, D_K, D_OUT)) + f64(b3)[:, None, :]
    return out.mean(axis=0)

@@ -1,0 +1,241 @@
+from contextlib import ExitStack
+
+import concourse.mybir as mybir
+from concourse.masks import make_identity
+
+F32 = mybir.dt.float32
+BF16 = mybir.dt.bfloat16
+I32 = mybir.dt.int32
+U32 = mybir.dt.uint32
+U8 = mybir.dt.uint8
+FP8X4 = mybir.dt.float8_e4m3fn_x4
+ADD = mybir.AluOpType.add
+MULT = mybir.AluOpType.mult
+RELU = mybir.ActivationFunctionType.Relu
+
+TREES, BATCH, D_H, D_K, D_OUT = 8, 256, 1024, 1024, 256
+P = 128
+K_PASS = 4 * P
+PASSES = D_H // K_PASS
+ROW_TILES = BATCH // P
+WORDS = K_PASS // 2
+N_L1 = 512
+SHARE = 4
+
+FLOPS = 2 * TREES * BATCH * (D_H * D_K + D_K * D_OUT)
+
+
+def load_scale_planes(nc, planes, scales, first_pass):
+    for quad in range(4):
+        nc.sync.dma_start(
+            out=planes[32 * quad : 32 * quad + 4 * SHARE, :].bitcast(I32),
+            in_=scales[first_pass : first_pass + SHARE, 4 * quad : 4 * quad + 4, :].bitcast(I32),
+        )
+
+
+def tile_randomforestmlp_pa_e_kernel(
+    tc, h1, w2_words, w2_scales, b2, w3_words, w3_scales, b3, out
+):
+    nc = tc.nc
+    groups = TREES * PASSES // SHARE
+    with ExitStack() as ctx:
+        ctx.enter_context(tc.manual_schedule())
+        keep = ctx.enter_context(tc.tile_pool(name="keep", bufs=1))
+        work = ctx.enter_context(tc.tile_pool(name="work", bufs=2))
+        sums = ctx.enter_context(tc.psum_pool(name="sums", bufs=4))
+        turns = ctx.enter_context(tc.psum_pool(name="turns", bufs=4))
+
+        h1_sb = [keep.tile([P, ROW_TILES, D_H], BF16, name="h1_sb%d" % t) for t in range(TREES)]
+        w2_sb = [
+            keep.tile([P, PASSES, D_K], U32, name="w2_sb%d" % t, align_bytes=64)
+            for t in range(TREES)
+        ]
+        w3_sb = [
+            keep.tile([P, SHARE, D_OUT], U32, name="w3_sb%d" % s, align_bytes=64)
+            for s in range(groups)
+        ]
+        w2_planes = [
+            keep.tile([P, D_K], U8, name="w2_planes%d" % s, align_bytes=64) for s in range(groups)
+        ]
+        w3_planes = [
+            keep.tile([P, D_OUT], U8, name="w3_planes%d" % s, align_bytes=64)
+            for s in range(groups)
+        ]
+        h2_codes = [
+            keep.tile([P, PASSES, BATCH], U32, name="h2_codes%d" % t, align_bytes=64)
+            for t in range(TREES)
+        ]
+        h2_scales = [
+            keep.tile([P, PASSES, BATCH], U8, name="h2_scales%d" % t, align_bytes=64)
+            for t in range(TREES)
+        ]
+        b2_rows = keep.tile([P, D_K], BF16)
+        b3_rows = keep.tile([P, D_OUT], BF16)
+        eighth = keep.tile([P, P], BF16)
+        ident_f32 = keep.tile([P, P], F32)
+        ident_bf16 = keep.tile([P, P], BF16)
+        b3_mean = keep.tile([P, D_OUT], F32)
+        out_sb = keep.tile([P, ROW_TILES, D_OUT], F32)
+
+        nc.vector.memset(b2_rows[:], 0.0)
+        nc.vector.memset(w2_planes[0][:].bitcast(I32), 0)
+        nc.vector.memset(b3_rows[:], 0.0)
+        nc.vector.memset(eighth[:], 1.0 / TREES)
+        for s in range(groups):
+            if s > 0:
+                nc.vector.memset(w2_planes[s][:].bitcast(I32), 0)
+            nc.vector.memset(w3_planes[s][:].bitcast(I32), 0)
+        make_identity(nc, ident_bf16[:])
+        make_identity(nc, ident_f32[:])
+
+        nc.scalar.dma_start(out=b2_rows[0:TREES, :], in_=b2)
+        nc.scalar.dma_start(out=b3_rows[0:TREES, :], in_=b3)
+        for t in range(TREES):
+            nc.sync.dma_start(out=h1_sb[t][:], in_=h1[t].rearrange("(p i) k -> p i k", i=ROW_TILES))
+            first_pass = t * PASSES
+            if first_pass % SHARE == 0:
+                load_scale_planes(nc, w2_planes[first_pass // SHARE], w2_scales, first_pass)
+            else:
+                s = first_pass // SHARE
+                load_scale_planes(nc, w3_planes[s], w3_scales, s * SHARE)
+            nc.sync.dma_start(
+                out=w2_sb[t][:].bitcast(I32),
+                in_=w2_words[first_pass : first_pass + PASSES]
+                .rearrange("g p n j -> p g (n j)")
+                .bitcast(I32),
+            )
+        for s in range(groups):
+            nc.sync.dma_start(
+                out=w3_sb[s][:].bitcast(I32),
+                in_=w3_words[s * SHARE : (s + 1) * SHARE]
+                .rearrange("g p n j -> p g (n j)")
+                .bitcast(I32),
+            )
+
+        def turn(words_of):
+            turned = turns.tile([P, 2, BATCH], F32, tag="turn", name="turned")
+            for u in range(2):
+                for i in range(ROW_TILES):
+                    nc.tensor.transpose(turned[:, u, i * P : (i + 1) * P], words_of(i, u), ident_f32[:])
+            return turned
+
+        def spread_b2(t):
+            spread = turns.tile([P, D_K], BF16, tag="turn", name="spread")
+            for h in range(D_K // N_L1):
+                cols = slice(h * N_L1, (h + 1) * N_L1)
+                nc.tensor.matmul(
+                    spread[:, cols],
+                    lhsT=ident_bf16[:, t : t + 1].to_broadcast([P, P]),
+                    rhs=b2_rows[:, cols],
+                    start=True,
+                    stop=True,
+                )
+            b2_all = work.tile([P, D_K], BF16, name="b2_all")
+            nc.scalar.copy(out=b2_all[:], in_=spread[:])
+            return b2_all
+
+        def turn_and_quantise_h1(t):
+            h1_words = h1_sb[t][:].bitcast(F32)
+            grouped = work.tile([P, PASSES, 4 * BATCH], BF16, name="h1_grouped", align_bytes=64)
+            codes = work.tile([P, PASSES, BATCH], U32, name="h1_codes", align_bytes=64)
+            scales = work.tile([P, PASSES, BATCH], U8, name="h1_scales", align_bytes=64)
+            for g in range(PASSES):
+                turned = turn(lambda i, u: h1_words[:, i, g * WORDS + u : (g + 1) * WORDS : 2])
+                nc.scalar.copy(
+                    out=grouped[:, g, :].bitcast(F32).rearrange("p (c u) -> p c u", u=2),
+                    in_=turned[:].rearrange("p u c -> p c u"),
+                )
+                nc.vector.quantize_mx(
+                    out=codes[:, g, :].bitcast(FP8X4), scales=scales[:, g, :], in_=grouped[:, g, :]
+                )
+            return codes, scales
+
+        def layer1(t, codes, scales, b2_all):
+            h2_pre = work.tile([P, ROW_TILES, PASSES, K_PASS], BF16, name="h2_pre")
+            for h in range(D_K // N_L1):
+                cols = slice(h * N_L1, (h + 1) * N_L1)
+                for i in range(ROW_TILES):
+                    rows = slice(i * P, (i + 1) * P)
+                    acc = sums.tile([P, N_L1], F32, tag="sum", name="acc")
+                    for g in range(PASSES):
+                        s, place = divmod(t * PASSES + g, SHARE)
+                        nc.tensor.matmul_mx(
+                            out=acc[:],
+                            lhsT=codes[:, g, rows].bitcast(FP8X4),
+                            lhsT_scale=scales[:, g, rows],
+                            rhs=w2_sb[t][:, g, cols].bitcast(FP8X4),
+                            rhs_scale=w2_planes[s][4 * place : P, cols],
+                            start=(g == 0),
+                            stop=(g == PASSES - 1),
+                        )
+                    nc.vector.tensor_tensor(
+                        out=h2_pre[:, i, h, :].rearrange("r (u p e) -> r p u e", u=2, e=2),
+                        in0=acc[:].rearrange("r (p u e) -> r p u e", u=2, e=2),
+                        in1=b2_all[:, cols].rearrange("r (p u e) -> r p u e", u=2, e=2),
+                        op=ADD,
+                    )
+            return h2_pre
+
+        def turn_h2(h2_pre):
+            h2_words = h2_pre[:].bitcast(F32)
+            grouped = work.tile([P, PASSES, 4 * BATCH], BF16, name="h2_grouped", align_bytes=64)
+            for g in range(PASSES):
+                turned = turn(lambda i, u: h2_words[:, i, g, u * P : (u + 1) * P])
+                nc.scalar.activation(
+                    out=grouped[:, g, :].rearrange("p (c u e) -> p c u e", u=2, e=2),
+                    in_=turned[:].bitcast(BF16).rearrange("p u (c e) -> p c u e", e=2),
+                    func=RELU,
+                )
+            return grouped
+
+        def quantise_h2(t, grouped):
+            for g in range(PASSES):
+                nc.vector.quantize_mx(
+                    out=h2_codes[t][:, g, :].bitcast(FP8X4),
+                    scales=h2_scales[t][:, g, :],
+                    in_=grouped[:, g, :],
+                )
+
+        mean_ps = turns.tile([P, D_OUT], F32, tag="turn", name="mean_ps")
+        nc.tensor.matmul(mean_ps[:], lhsT=eighth[:], rhs=b3_rows[:], start=True, stop=True)
+        nc.scalar.copy(out=b3_mean[:], in_=mean_ps[:])
+
+        b2_all = spread_b2(0)
+        codes, scales = turn_and_quantise_h1(0)
+        grouped = None
+        for t in range(TREES):
+            h2_pre = layer1(t, codes, scales, b2_all)
+            if t > 0:
+                quantise_h2(t - 1, grouped)
+            if t + 1 < TREES:
+                codes, scales = turn_and_quantise_h1(t + 1)
+                b2_all = spread_b2(t + 1)
+            grouped = turn_h2(h2_pre)
+        quantise_h2(TREES - 1, grouped)
+
+        out_acc = [sums.tile([P, D_OUT], F32, tag="sum", name="out_acc%d" % i) for i in range(ROW_TILES)]
+        last = TREES * PASSES - 1
+        for step in range(TREES * PASSES):
+            t, g = divmod(step, PASSES)
+            s, place = divmod(step, SHARE)
+            for i in range(ROW_TILES):
+                rows = slice(i * P, (i + 1) * P)
+                nc.tensor.matmul_mx(
+                    out=out_acc[i][:],
+                    lhsT=h2_codes[t][:, g, rows].bitcast(FP8X4),
+                    lhsT_scale=h2_scales[t][:, g, rows],
+                    rhs=w3_sb[s][:, place, :].bitcast(FP8X4),
+                    rhs_scale=w3_planes[s][4 * place : P, :],
+                    start=(step == 0),
+                    stop=(step == last),
+                )
+        for i in range(ROW_TILES):
+            nc.vector.scalar_tensor_tensor(
+                out=out_sb[:, i, :],
+                in0=out_acc[i][:],
+                scalar=1.0 / TREES,
+                in1=b3_mean[:],
+                op0=MULT,
+                op1=ADD,
+            )
+        nc.sync.dma_start(out=out.rearrange("(p i) d -> p i d", i=ROW_TILES), in_=out_sb[:])

@@ -15,11 +15,11 @@ RELU = mybir.ActivationFunctionType.Relu
 
 TREES, BATCH, D_H, D_K, D_OUT = 8, 256, 1024, 1024, 256
 P = 128
-K_PASS = 4 * P
+PACK = 4
+K_PASS = PACK * P
 PASSES = D_H // K_PASS
 ROW_TILES = BATCH // P
 WORDS = K_PASS // 2
-N_L1 = 512
 SHARE = 4
 
 FLOPS = 2 * TREES * BATCH * (D_H * D_K + D_K * D_OUT)
@@ -42,18 +42,21 @@ def tile_randomforestmlp_pa_e_kernel(
         ctx.enter_context(tc.manual_schedule())
         keep = ctx.enter_context(tc.tile_pool(name="keep", bufs=1))
         work = ctx.enter_context(tc.tile_pool(name="work", bufs=2))
-        sums = ctx.enter_context(tc.psum_pool(name="sums", bufs=4))
-        turns = ctx.enter_context(tc.psum_pool(name="turns", bufs=4))
+        sorted_pool = ctx.enter_context(tc.tile_pool(name="sorted", bufs=3))
+        outs = ctx.enter_context(tc.psum_pool(name="outs", bufs=1))
+        accs = ctx.enter_context(tc.psum_pool(name="accs", bufs=3))
+        turns = ctx.enter_context(tc.psum_pool(name="turns", bufs=3))
 
-        h1_sb = [keep.tile([P, ROW_TILES, D_H], BF16, name="h1_sb%d" % t) for t in range(TREES)]
-        w2_sb = [
-            keep.tile([P, PASSES, D_K], U32, name="w2_sb%d" % t, align_bytes=64)
-            for t in range(TREES)
+        h1_sb = [keep.tile([P, ROW_TILES, D_H], BF16, name="h1_sb%d" % e) for e in range(TREES)]
+        w2_raw = [
+            [keep.tile([P, PASSES, K_PASS], U32, name="w2_raw%d_%d" % (e, h)) for h in range(PASSES)]
+            for e in range(TREES)
         ]
         w3_sb = [
             keep.tile([P, SHARE, D_OUT], U32, name="w3_sb%d" % s, align_bytes=64)
             for s in range(groups)
         ]
+        w2_planes_raw = [keep.tile([P, D_K], U8, name="w2_planes_raw%d" % s) for s in range(groups)]
         w2_planes = [
             keep.tile([P, D_K], U8, name="w2_planes%d" % s, align_bytes=64) for s in range(groups)
         ]
@@ -61,174 +64,199 @@ def tile_randomforestmlp_pa_e_kernel(
             keep.tile([P, D_OUT], U8, name="w3_planes%d" % s, align_bytes=64)
             for s in range(groups)
         ]
-        h2_codes = [
-            keep.tile([P, PASSES, BATCH], U32, name="h2_codes%d" % t, align_bytes=64)
-            for t in range(TREES)
-        ]
-        h2_scales = [
-            keep.tile([P, PASSES, BATCH], U8, name="h2_scales%d" % t, align_bytes=64)
-            for t in range(TREES)
-        ]
         b2_rows = keep.tile([P, D_K], BF16)
         b3_rows = keep.tile([P, D_OUT], BF16)
         eighth = keep.tile([P, P], BF16)
         ident_f32 = keep.tile([P, P], F32)
         ident_bf16 = keep.tile([P, P], BF16)
+        b2_cols = keep.tile([P, PASSES * PACK, TREES], F32)
         b3_mean = keep.tile([P, D_OUT], F32)
         out_sb = keep.tile([P, ROW_TILES, D_OUT], F32)
 
         nc.vector.memset(b2_rows[:], 0.0)
-        nc.vector.memset(w2_planes[0][:].bitcast(I32), 0)
+        nc.vector.memset(w2_planes_raw[0][:].bitcast(I32), 0)
         nc.vector.memset(b3_rows[:], 0.0)
         nc.vector.memset(eighth[:], 1.0 / TREES)
         for s in range(groups):
             if s > 0:
-                nc.vector.memset(w2_planes[s][:].bitcast(I32), 0)
+                nc.vector.memset(w2_planes_raw[s][:].bitcast(I32), 0)
             nc.vector.memset(w3_planes[s][:].bitcast(I32), 0)
         make_identity(nc, ident_bf16[:])
         make_identity(nc, ident_f32[:])
 
         nc.scalar.dma_start(out=b2_rows[0:TREES, :], in_=b2)
         nc.scalar.dma_start(out=b3_rows[0:TREES, :], in_=b3)
-        for t in range(TREES):
-            nc.sync.dma_start(out=h1_sb[t][:], in_=h1[t].rearrange("(p i) k -> p i k", i=ROW_TILES))
-            first_pass = t * PASSES
+        for e in range(TREES):
+            first_pass = e * PASSES
+            s = first_pass // SHARE
+            nc.sync.dma_start(out=h1_sb[e][:], in_=h1[e].rearrange("(p i) k -> p i k", i=ROW_TILES))
             if first_pass % SHARE == 0:
-                load_scale_planes(nc, w2_planes[first_pass // SHARE], w2_scales, first_pass)
-            else:
-                s = first_pass // SHARE
-                load_scale_planes(nc, w3_planes[s], w3_scales, s * SHARE)
-            nc.sync.dma_start(
-                out=w2_sb[t][:].bitcast(I32),
-                in_=w2_words[first_pass : first_pass + PASSES]
-                .rearrange("g p n j -> p g (n j)")
-                .bitcast(I32),
-            )
-        for s in range(groups):
-            nc.sync.dma_start(
-                out=w3_sb[s][:].bitcast(I32),
-                in_=w3_words[s * SHARE : (s + 1) * SHARE]
-                .rearrange("g p n j -> p g (n j)")
-                .bitcast(I32),
-            )
-
-        def turn(words_of):
-            turned = turns.tile([P, 2, BATCH], F32, tag="turn", name="turned")
-            for u in range(2):
-                for i in range(ROW_TILES):
-                    nc.tensor.transpose(turned[:, u, i * P : (i + 1) * P], words_of(i, u), ident_f32[:])
-            return turned
-
-        def spread_b2(t):
-            spread = turns.tile([P, D_K], BF16, tag="turn", name="spread")
-            for h in range(D_K // N_L1):
-                cols = slice(h * N_L1, (h + 1) * N_L1)
-                nc.tensor.matmul(
-                    spread[:, cols],
-                    lhsT=ident_bf16[:, t : t + 1].to_broadcast([P, P]),
-                    rhs=b2_rows[:, cols],
-                    start=True,
-                    stop=True,
+                load_scale_planes(nc, w2_planes_raw[s], w2_scales, first_pass)
+            for h in range(PASSES):
+                nc.sync.dma_start(
+                    out=w2_raw[e][h][:].bitcast(I32),
+                    in_=w2_words[first_pass : first_pass + PASSES, :, h * K_PASS : (h + 1) * K_PASS, :]
+                    .rearrange("g p n j -> p g (n j)")
+                    .bitcast(I32),
                 )
-            b2_all = work.tile([P, D_K], BF16, name="b2_all")
-            nc.scalar.copy(out=b2_all[:], in_=spread[:])
-            return b2_all
-
-        def turn_and_quantise_h1(t):
-            h1_words = h1_sb[t][:].bitcast(F32)
-            grouped = work.tile([P, PASSES, 4 * BATCH], BF16, name="h1_grouped", align_bytes=64)
-            codes = work.tile([P, PASSES, BATCH], U32, name="h1_codes", align_bytes=64)
-            scales = work.tile([P, PASSES, BATCH], U8, name="h1_scales", align_bytes=64)
-            for g in range(PASSES):
-                turned = turn(lambda i, u: h1_words[:, i, g * WORDS + u : (g + 1) * WORDS : 2])
-                nc.scalar.copy(
-                    out=grouped[:, g, :].bitcast(F32).rearrange("p (c u) -> p c u", u=2),
-                    in_=turned[:].rearrange("p u c -> p c u"),
+            if first_pass % SHARE == 0:
+                load_scale_planes(nc, w3_planes[s], w3_scales, first_pass)
+                nc.sync.dma_start(
+                    out=w3_sb[s][:].bitcast(I32),
+                    in_=w3_words[first_pass : first_pass + SHARE]
+                    .rearrange("g p n j -> p g (n j)")
+                    .bitcast(I32),
                 )
-                nc.vector.quantize_mx(
-                    out=codes[:, g, :].bitcast(FP8X4), scales=scales[:, g, :], in_=grouped[:, g, :]
-                )
-            return codes, scales
 
-        def layer1(t, codes, scales, b2_all):
-            h2_pre = work.tile([P, ROW_TILES, PASSES, K_PASS], BF16, name="h2_pre")
-            for h in range(D_K // N_L1):
-                cols = slice(h * N_L1, (h + 1) * N_L1)
-                for i in range(ROW_TILES):
-                    rows = slice(i * P, (i + 1) * P)
-                    acc = sums.tile([P, N_L1], F32, tag="sum", name="acc")
-                    for g in range(PASSES):
-                        s, place = divmod(t * PASSES + g, SHARE)
-                        nc.tensor.matmul_mx(
-                            out=acc[:],
-                            lhsT=codes[:, g, rows].bitcast(FP8X4),
-                            lhsT_scale=scales[:, g, rows],
-                            rhs=w2_sb[t][:, g, cols].bitcast(FP8X4),
-                            rhs_scale=w2_planes[s][4 * place : P, cols],
-                            start=(g == 0),
-                            stop=(g == PASSES - 1),
-                        )
-                    nc.vector.tensor_tensor(
-                        out=h2_pre[:, i, h, :].rearrange("r (u p e) -> r p u e", u=2, e=2),
-                        in0=acc[:].rearrange("r (p u e) -> r p u e", u=2, e=2),
-                        in1=b2_all[:, cols].rearrange("r (p u e) -> r p u e", u=2, e=2),
-                        op=ADD,
-                    )
-            return h2_pre
-
-        def turn_h2(h2_pre):
-            h2_words = h2_pre[:].bitcast(F32)
-            grouped = work.tile([P, PASSES, 4 * BATCH], BF16, name="h2_grouped", align_bytes=64)
-            for g in range(PASSES):
-                turned = turn(lambda i, u: h2_words[:, i, g, u * P : (u + 1) * P])
-                nc.scalar.activation(
-                    out=grouped[:, g, :].rearrange("p (c u e) -> p c u e", u=2, e=2),
-                    in_=turned[:].bitcast(BF16).rearrange("p u (c e) -> p c u e", e=2),
-                    func=RELU,
+        b2_turned = turns.tile([P, PASSES * PACK, P], BF16, tag="turn", name="b2_turned")
+        for h in range(PASSES):
+            for j in range(PACK):
+                nc.tensor.transpose(
+                    b2_turned[:, h * PACK + j, :],
+                    b2_rows[:, h * K_PASS + j : (h + 1) * K_PASS : PACK],
+                    ident_bf16[:],
                 )
-            return grouped
-
-        def quantise_h2(t, grouped):
-            for g in range(PASSES):
-                nc.vector.quantize_mx(
-                    out=h2_codes[t][:, g, :].bitcast(FP8X4),
-                    scales=h2_scales[t][:, g, :],
-                    in_=grouped[:, g, :],
-                )
+        nc.scalar.copy(out=b2_cols[:], in_=b2_turned[:, :, 0:TREES])
 
         mean_ps = turns.tile([P, D_OUT], F32, tag="turn", name="mean_ps")
         nc.tensor.matmul(mean_ps[:], lhsT=eighth[:], rhs=b3_rows[:], start=True, stop=True)
         nc.scalar.copy(out=b3_mean[:], in_=mean_ps[:])
 
-        b2_all = spread_b2(0)
-        codes, scales = turn_and_quantise_h1(0)
-        grouped = None
-        for t in range(TREES):
-            h2_pre = layer1(t, codes, scales, b2_all)
-            if t > 0:
-                quantise_h2(t - 1, grouped)
-            if t + 1 < TREES:
-                codes, scales = turn_and_quantise_h1(t + 1)
-                b2_all = spread_b2(t + 1)
-            grouped = turn_h2(h2_pre)
-        quantise_h2(TREES - 1, grouped)
-
-        out_acc = [sums.tile([P, D_OUT], F32, tag="sum", name="out_acc%d" % i) for i in range(ROW_TILES)]
-        last = TREES * PASSES - 1
-        for step in range(TREES * PASSES):
-            t, g = divmod(step, PASSES)
-            s, place = divmod(step, SHARE)
-            for i in range(ROW_TILES):
-                rows = slice(i * P, (i + 1) * P)
-                nc.tensor.matmul_mx(
-                    out=out_acc[i][:],
-                    lhsT=h2_codes[t][:, g, rows].bitcast(FP8X4),
-                    lhsT_scale=h2_scales[t][:, g, rows],
-                    rhs=w3_sb[s][:, place, :].bitcast(FP8X4),
-                    rhs_scale=w3_planes[s][4 * place : P, :],
-                    start=(step == 0),
-                    stop=(step == last),
+        def turn_h1(e):
+            h1_words = h1_sb[e][:].bitcast(F32)
+            grouped = work.tile([P, PASSES, PACK * BATCH], BF16, name="h1_grouped", align_bytes=64)
+            for g in range(PASSES):
+                turned = turns.tile([P, 2, BATCH], F32, tag="turn", name="turned")
+                for u in range(2):
+                    for i in range(ROW_TILES):
+                        nc.tensor.transpose(
+                            turned[:, u, i * P : (i + 1) * P],
+                            h1_words[:, i, g * WORDS + u : (g + 1) * WORDS : 2],
+                            ident_f32[:],
+                        )
+                nc.scalar.copy(
+                    out=grouped[:, g, :].bitcast(F32).rearrange("p (c u) -> p c u", u=2),
+                    in_=turned[:].rearrange("p u c -> p c u"),
                 )
+            return grouped
+
+        def quantise_h1(grouped):
+            codes = work.tile([P, PASSES, BATCH], U32, name="h1_codes", align_bytes=64)
+            scales = work.tile([P, PASSES, BATCH], U8, name="h1_scales", align_bytes=64)
+            for g in range(PASSES):
+                nc.vector.quantize_mx(
+                    out=codes[:, g, :].bitcast(FP8X4), scales=scales[:, g, :], in_=grouped[:, g, :]
+                )
+            return codes, scales
+
+        def sort_planes(s):
+            nc.vector.tensor_copy(
+                out=w2_planes[s][:].rearrange("p (h j m) -> p h m j", h=PASSES, j=PACK),
+                in_=w2_planes_raw[s][:].rearrange("p (h m j) -> p h m j", h=PASSES, j=PACK),
+            )
+
+        def sort_w2(e):
+            halves = []
+            for h in range(PASSES):
+                half = sorted_pool.tile(
+                    [P, PASSES, PACK, P], U32, name="w2_sorted%d" % h, align_bytes=64
+                )
+                nc.vector.tensor_copy(
+                    out=half[:].bitcast(I32),
+                    in_=w2_raw[e][h][:].bitcast(I32).rearrange("p g (m j) -> p g j m", j=PACK),
+                )
+                halves.append(half)
+            return halves
+
+        def layer1(e, h, halves, codes, scales, h2_rows):
+            for pair in range(PACK // 2):
+                acc = accs.tile([P, 2, BATCH], F32, tag="acc", name="acc")
+                for v in range(2):
+                    j = 2 * pair + v
+                    for g in range(PASSES):
+                        s, place = divmod(e * PASSES + g, SHARE)
+                        cols = slice(h * K_PASS + j * P, h * K_PASS + (j + 1) * P)
+                        nc.tensor.matmul_mx(
+                            out=acc[:, v, :],
+                            lhsT=halves[h][:, g, j, :].bitcast(FP8X4),
+                            lhsT_scale=w2_planes[s][4 * place : P, cols],
+                            rhs=codes[:, g, :].bitcast(FP8X4),
+                            rhs_scale=scales[:, g, :],
+                            start=(g == 0),
+                            stop=(g == PASSES - 1),
+                        )
+                for v in range(2):
+                    j = 2 * pair + v
+                    nc.scalar.activation(
+                        out=h2_rows[:, h, j, :],
+                        in_=acc[:, v, :],
+                        func=RELU,
+                        bias=b2_cols[:, h * PACK + j, e : e + 1],
+                    )
+
+        def interleave_h2(h, h2_rows, grouped):
+            nc.vector.tensor_copy(
+                out=grouped[:, h, :].rearrange("p (c j) -> p c j", j=PACK),
+                in_=h2_rows[:, h, :, :].rearrange("p j c -> p c j"),
+            )
+
+        def quantise_h2(h, grouped, codes, scales):
+            nc.vector.quantize_mx(
+                out=codes[:, h, :].bitcast(FP8X4), scales=scales[:, h, :], in_=grouped[:, h, :]
+            )
+
+        out_acc = [outs.tile([P, D_OUT], F32, name="out_acc%d" % i) for i in range(ROW_TILES)]
+        last = TREES * PASSES - 1
+
+        def layer2(e, codes, scales):
+            for h in range(PASSES):
+                step = e * PASSES + h
+                s, place = divmod(step, SHARE)
+                for i in range(ROW_TILES):
+                    rows = slice(i * P, (i + 1) * P)
+                    nc.tensor.matmul_mx(
+                        out=out_acc[i][:],
+                        lhsT=codes[:, h, rows].bitcast(FP8X4),
+                        lhsT_scale=scales[:, h, rows],
+                        rhs=w3_sb[s][:, place, :].bitcast(FP8X4),
+                        rhs_scale=w3_planes[s][4 * place : P, :],
+                        start=(step == 0),
+                        stop=(step == last),
+                    )
+
+        h1_grouped = turn_h1(0)
+        sort_planes(0)
+        halves = sort_w2(0)
+        h1_codes, h1_scales = quantise_h1(h1_grouped)
+        before = None
+        for e in range(TREES):
+            more = e + 1 < TREES
+            if more:
+                h1_grouped = turn_h1(e + 1)
+            if before is not None:
+                quantise_h2(1, before[0], before[1], before[2])
+            if more:
+                if (e + 1) * PASSES % SHARE == 0:
+                    sort_planes((e + 1) * PASSES // SHARE)
+                next_halves = sort_w2(e + 1)
+                next_codes, next_scales = quantise_h1(h1_grouped)
+            h2_rows = work.tile([P, PASSES, PACK, BATCH], BF16, name="h2_rows")
+            h2_grouped = work.tile([P, PASSES, PACK * BATCH], BF16, name="h2_grouped", align_bytes=64)
+            h2_codes = work.tile([P, PASSES, BATCH], U32, name="h2_codes", align_bytes=64)
+            h2_scales = work.tile([P, PASSES, BATCH], U8, name="h2_scales", align_bytes=64)
+            layer1(e, 0, halves, h1_codes, h1_scales, h2_rows)
+            interleave_h2(0, h2_rows, h2_grouped)
+            layer1(e, 1, halves, h1_codes, h1_scales, h2_rows)
+            if before is not None:
+                layer2(e - 1, before[1], before[2])
+            quantise_h2(0, h2_grouped, h2_codes, h2_scales)
+            interleave_h2(1, h2_rows, h2_grouped)
+            before = (h2_grouped, h2_codes, h2_scales)
+            if more:
+                halves, h1_codes, h1_scales = next_halves, next_codes, next_scales
+        quantise_h2(1, before[0], before[1], before[2])
+        layer2(TREES - 1, before[1], before[2])
+
         for i in range(ROW_TILES):
             nc.vector.scalar_tensor_tensor(
                 out=out_sb[:, i, :],

@@ -162,8 +162,8 @@ def tile_randomforestmlp_pa_e_kernel(
                     [P, PASSES, PACK, P], U32, name="w2_sorted%d" % h, align_bytes=64
                 )
                 nc.vector.tensor_copy(
-                    out=half[:].bitcast(I32),
-                    in_=w2_raw[e][h][:].bitcast(I32).rearrange("p g (m j) -> p g j m", j=PACK),
+                    out=half[:].bitcast(I32).rearrange("p g j m -> p g m j"),
+                    in_=w2_raw[e][h][:].bitcast(I32).rearrange("p g (m j) -> p g m j", j=PACK),
                 )
                 halves.append(half)
             return halves

@@ -86,6 +86,15 @@ def tile_randomforestmlp_pa_e_kernel(
 
         nc.scalar.dma_start(out=b2_rows[0:TREES, :], in_=b2)
         nc.scalar.dma_start(out=b3_rows[0:TREES, :], in_=b3)
+        def load_w3(s):
+            load_scale_planes(nc, w3_planes[s], w3_scales, s * SHARE)
+            nc.sync.dma_start(
+                out=w3_sb[s][:].bitcast(I32),
+                in_=w3_words[s * SHARE : (s + 1) * SHARE]
+                .rearrange("g p n j -> p g (n j)")
+                .bitcast(I32),
+            )
+
         for e in range(TREES):
             first_pass = e * PASSES
             s = first_pass // SHARE
@@ -99,14 +108,9 @@ def tile_randomforestmlp_pa_e_kernel(
                     .rearrange("g p n j -> p g (n j)")
                     .bitcast(I32),
                 )
-            if first_pass % SHARE == 0:
-                load_scale_planes(nc, w3_planes[s], w3_scales, first_pass)
-                nc.sync.dma_start(
-                    out=w3_sb[s][:].bitcast(I32),
-                    in_=w3_words[first_pass : first_pass + SHARE]
-                    .rearrange("g p n j -> p g (n j)")
-                    .bitcast(I32),
-                )
+            if first_pass % SHARE == 0 and s > 0:
+                load_w3(s - 1)
+        load_w3(groups - 1)
 
         b2_turned = turns.tile([P, PASSES * PACK, P], BF16, tag="turn", name="b2_turned")
         for h in range(PASSES):
@@ -154,19 +158,6 @@ def tile_randomforestmlp_pa_e_kernel(
                 out=w2_planes[s][:].rearrange("p (h j m) -> p h m j", h=PASSES, j=PACK),
                 in_=w2_planes_raw[s][:].rearrange("p (h m j) -> p h m j", h=PASSES, j=PACK),
             )
-
-        def sort_w2(e):
-            halves = []
-            for h in range(PASSES):
-                half = sorted_pool.tile(
-                    [P, PASSES, PACK, P], U32, name="w2_sorted%d" % h, align_bytes=64
-                )
-                nc.vector.tensor_copy(
-                    out=half[:].bitcast(I32).rearrange("p g j m -> p g m j"),
-                    in_=w2_raw[e][h][:].bitcast(I32).rearrange("p g (m j) -> p g m j", j=PACK),
-                )
-                halves.append(half)
-            return halves
 
         def layer1(e, h, halves, codes, scales, h2_rows):
             for pair in range(PACK // 2):
@@ -224,38 +215,55 @@ def tile_randomforestmlp_pa_e_kernel(
                         stop=(step == last),
                     )
 
+        def sort_half(e, h):
+            half = sorted_pool.tile([P, PASSES, PACK, P], U32, name="w2_sorted%d" % h, align_bytes=64)
+            nc.vector.tensor_copy(
+                out=half[:].bitcast(I32).rearrange("p g j m -> p g m j"),
+                in_=w2_raw[e][h][:].bitcast(I32).rearrange("p g (m j) -> p g m j", j=PACK),
+            )
+            return half
+
         h1_grouped = turn_h1(0)
         sort_planes(0)
-        halves = sort_w2(0)
+        halves = [sort_half(0, h) for h in range(PASSES)]
         h1_codes, h1_scales = quantise_h1(h1_grouped)
-        before = None
-        for e in range(TREES):
+        rows_before = None
+        for e in range(TREES + 1):
             more = e + 1 < TREES
             if more:
                 h1_grouped = turn_h1(e + 1)
-            if before is not None:
-                quantise_h2(1, before[0], before[1], before[2])
-            if more:
                 if (e + 1) * PASSES % SHARE == 0:
                     sort_planes((e + 1) * PASSES // SHARE)
-                next_halves = sort_w2(e + 1)
+            next_halves = []
+            if rows_before is not None:
+                h2_grouped = work.tile(
+                    [P, PASSES, PACK * BATCH], BF16, name="h2_grouped", align_bytes=64
+                )
+                h2_codes = work.tile([P, PASSES, BATCH], U32, name="h2_codes", align_bytes=64)
+                h2_scales = work.tile([P, PASSES, BATCH], U8, name="h2_scales", align_bytes=64)
+            if more:
+                for h in range(PASSES):
+                    if rows_before is not None:
+                        interleave_h2(h, rows_before, h2_grouped)
+                    next_halves.append(sort_half(e + 1, h))
+                    if rows_before is not None:
+                        quantise_h2(h, h2_grouped, h2_codes, h2_scales)
                 next_codes, next_scales = quantise_h1(h1_grouped)
-            h2_rows = work.tile([P, PASSES, PACK, BATCH], BF16, name="h2_rows")
-            h2_grouped = work.tile([P, PASSES, PACK * BATCH], BF16, name="h2_grouped", align_bytes=64)
-            h2_codes = work.tile([P, PASSES, BATCH], U32, name="h2_codes", align_bytes=64)
-            h2_scales = work.tile([P, PASSES, BATCH], U8, name="h2_scales", align_bytes=64)
-            layer1(e, 0, halves, h1_codes, h1_scales, h2_rows)
-            interleave_h2(0, h2_rows, h2_grouped)
-            layer1(e, 1, halves, h1_codes, h1_scales, h2_rows)
-            if before is not None:
-                layer2(e - 1, before[1], before[2])
-            quantise_h2(0, h2_grouped, h2_codes, h2_scales)
-            interleave_h2(1, h2_rows, h2_grouped)
-            before = (h2_grouped, h2_codes, h2_scales)
+            else:
+                for h in range(PASSES):
+                    interleave_h2(h, rows_before, h2_grouped)
+                for h in range(PASSES):
+                    quantise_h2(h, h2_grouped, h2_codes, h2_scales)
+            if e < TREES:
+                h2_rows = work.tile([P, PASSES, PACK, BATCH], BF16, name="h2_rows")
+                for h in range(PASSES):
+                    layer1(e, h, halves, h1_codes, h1_scales, h2_rows)
+            if rows_before is not None:
+                layer2(e - 1, h2_codes, h2_scales)
+            if e < TREES:
+                rows_before = h2_rows
             if more:
                 halves, h1_codes, h1_scales = next_halves, next_codes, next_scales
-        quantise_h2(1, before[0], before[1], before[2])
-        layer2(TREES - 1, before[1], before[2])
 
         for i in range(ROW_TILES):
             nc.vector.scalar_tensor_tensor(

@@ -43,9 +43,10 @@ def tile_randomforestmlp_pa_e_kernel(
         keep = ctx.enter_context(tc.tile_pool(name="keep", bufs=1))
         work = ctx.enter_context(tc.tile_pool(name="work", bufs=2))
         sorted_pool = ctx.enter_context(tc.tile_pool(name="sorted", bufs=3))
+        codes_pool = ctx.enter_context(tc.tile_pool(name="codes", bufs=3))
         outs = ctx.enter_context(tc.psum_pool(name="outs", bufs=1))
-        accs = ctx.enter_context(tc.psum_pool(name="accs", bufs=3))
-        turns = ctx.enter_context(tc.psum_pool(name="turns", bufs=3))
+        accs = ctx.enter_context(tc.psum_pool(name="accs", bufs=4))
+        turns = ctx.enter_context(tc.psum_pool(name="turns", bufs=2))
 
         h1_sb = [keep.tile([P, ROW_TILES, D_H], BF16, name="h1_sb%d" % e) for e in range(TREES)]
         w2_raw = [
@@ -147,10 +148,11 @@ def tile_randomforestmlp_pa_e_kernel(
         def quantise_h1(grouped):
             codes = work.tile([P, PASSES, BATCH], U32, name="h1_codes", align_bytes=64)
             scales = work.tile([P, PASSES, BATCH], U8, name="h1_scales", align_bytes=64)
-            for g in range(PASSES):
-                nc.vector.quantize_mx(
-                    out=codes[:, g, :].bitcast(FP8X4), scales=scales[:, g, :], in_=grouped[:, g, :]
-                )
+            nc.vector.quantize_mx(
+                out=codes[:].rearrange("p g c -> p (g c)").bitcast(FP8X4),
+                scales=scales[:].rearrange("p g c -> p (g c)"),
+                in_=grouped[:].rearrange("p g x -> p (g x)"),
+            )
             return codes, scales
 
         def sort_planes(s):
@@ -185,15 +187,17 @@ def tile_randomforestmlp_pa_e_kernel(
                         bias=b2_cols[:, h * PACK + j, e : e + 1],
                     )
 
-        def interleave_h2(h, h2_rows, grouped):
+        def interleave_h2(hs, h2_rows, grouped):
             nc.vector.tensor_copy(
-                out=grouped[:, h, :].rearrange("p (c j) -> p c j", j=PACK),
-                in_=h2_rows[:, h, :, :].rearrange("p j c -> p c j"),
+                out=grouped[:, hs, :].rearrange("p h (c j) -> p h c j", j=PACK),
+                in_=h2_rows[:, hs, :, :].rearrange("p h j c -> p h c j"),
             )
 
-        def quantise_h2(h, grouped, codes, scales):
+        def quantise_h2(hs, grouped, codes, scales):
             nc.vector.quantize_mx(
-                out=codes[:, h, :].bitcast(FP8X4), scales=scales[:, h, :], in_=grouped[:, h, :]
+                out=codes[:, hs, :].rearrange("p h c -> p (h c)").bitcast(FP8X4),
+                scales=scales[:, hs, :].rearrange("p h c -> p (h c)"),
+                in_=grouped[:, hs, :].rearrange("p h x -> p (h x)"),
             )
 
         out_acc = [outs.tile([P, D_OUT], F32, name="out_acc%d" % i) for i in range(ROW_TILES)]
@@ -228,40 +232,39 @@ def tile_randomforestmlp_pa_e_kernel(
         halves = [sort_half(0, h) for h in range(PASSES)]
         h1_codes, h1_scales = quantise_h1(h1_grouped)
         rows_before = None
-        for e in range(TREES + 1):
+        ready = None
+        for e in range(TREES + 2):
             more = e + 1 < TREES
+            quantised = None
             if more:
                 h1_grouped = turn_h1(e + 1)
                 if (e + 1) * PASSES % SHARE == 0:
                     sort_planes((e + 1) * PASSES // SHARE)
-            next_halves = []
             if rows_before is not None:
                 h2_grouped = work.tile(
                     [P, PASSES, PACK * BATCH], BF16, name="h2_grouped", align_bytes=64
                 )
-                h2_codes = work.tile([P, PASSES, BATCH], U32, name="h2_codes", align_bytes=64)
-                h2_scales = work.tile([P, PASSES, BATCH], U8, name="h2_scales", align_bytes=64)
+                h2_codes = codes_pool.tile([P, PASSES, BATCH], U32, name="h2_codes", align_bytes=64)
+                h2_scales = codes_pool.tile([P, PASSES, BATCH], U8, name="h2_scales", align_bytes=64)
+                steps = [slice(0, PASSES)] if e < TREES else [slice(h, h + 1) for h in range(PASSES)]
+                for hs in steps:
+                    interleave_h2(hs, rows_before, h2_grouped)
             if more:
-                for h in range(PASSES):
-                    if rows_before is not None:
-                        interleave_h2(h, rows_before, h2_grouped)
-                    next_halves.append(sort_half(e + 1, h))
-                    if rows_before is not None:
-                        quantise_h2(h, h2_grouped, h2_codes, h2_scales)
+                next_halves = [sort_half(e + 1, h) for h in range(PASSES)]
                 next_codes, next_scales = quantise_h1(h1_grouped)
-            else:
-                for h in range(PASSES):
-                    interleave_h2(h, rows_before, h2_grouped)
-                for h in range(PASSES):
-                    quantise_h2(h, h2_grouped, h2_codes, h2_scales)
+            if rows_before is not None:
+                for hs in steps:
+                    quantise_h2(hs, h2_grouped, h2_codes, h2_scales)
+                quantised = (h2_codes, h2_scales)
+            rows_before = None
             if e < TREES:
                 h2_rows = work.tile([P, PASSES, PACK, BATCH], BF16, name="h2_rows")
                 for h in range(PASSES):
                     layer1(e, h, halves, h1_codes, h1_scales, h2_rows)
-            if rows_before is not None:
-                layer2(e - 1, h2_codes, h2_scales)
-            if e < TREES:
                 rows_before = h2_rows
+            if ready is not None:
+                layer2(e - 2, ready[0], ready[1])
+            ready = quantised
             if more:
                 halves, h1_codes, h1_scales = next_halves, next_codes, next_scales
 

@@ -21,6 +21,7 @@ PASSES = D_H // K_PASS
 ROW_TILES = BATCH // P
 WORDS = K_PASS // 2
 SHARE = 4
+EARLY_GROUPS = 2
 
 FLOPS = 2 * TREES * BATCH * (D_H * D_K + D_K * D_OUT)
 
@@ -43,7 +44,6 @@ def tile_randomforestmlp_pa_e_kernel(
         keep = ctx.enter_context(tc.tile_pool(name="keep", bufs=1))
         work = ctx.enter_context(tc.tile_pool(name="work", bufs=2))
         sorted_pool = ctx.enter_context(tc.tile_pool(name="sorted", bufs=3))
-        codes_pool = ctx.enter_context(tc.tile_pool(name="codes", bufs=3))
         outs = ctx.enter_context(tc.psum_pool(name="outs", bufs=1))
         accs = ctx.enter_context(tc.psum_pool(name="accs", bufs=4))
         turns = ctx.enter_context(tc.psum_pool(name="turns", bufs=2))
@@ -109,9 +109,10 @@ def tile_randomforestmlp_pa_e_kernel(
                     .rearrange("g p n j -> p g (n j)")
                     .bitcast(I32),
                 )
-            if first_pass % SHARE == 0 and s > 0:
+            if first_pass % SHARE == 0 and 0 < s <= EARLY_GROUPS:
                 load_w3(s - 1)
-        load_w3(groups - 1)
+        for s in range(EARLY_GROUPS, groups):
+            load_w3(s)
 
         b2_turned = turns.tile([P, PASSES * PACK, P], BF16, tag="turn", name="b2_turned")
         for h in range(PASSES):
@@ -233,6 +234,7 @@ def tile_randomforestmlp_pa_e_kernel(
         h1_codes, h1_scales = quantise_h1(h1_grouped)
         rows_before = None
         ready = None
+        held = []
         for e in range(TREES + 2):
             more = e + 1 < TREES
             quantised = None
@@ -244,8 +246,8 @@ def tile_randomforestmlp_pa_e_kernel(
                 h2_grouped = work.tile(
                     [P, PASSES, PACK * BATCH], BF16, name="h2_grouped", align_bytes=64
                 )
-                h2_codes = codes_pool.tile([P, PASSES, BATCH], U32, name="h2_codes", align_bytes=64)
-                h2_scales = codes_pool.tile([P, PASSES, BATCH], U8, name="h2_scales", align_bytes=64)
+                h2_codes = keep.tile([P, PASSES, BATCH], U32, name="h2_codes%d" % e, align_bytes=64)
+                h2_scales = keep.tile([P, PASSES, BATCH], U8, name="h2_scales%d" % e, align_bytes=64)
                 steps = [slice(0, PASSES)] if e < TREES else [slice(h, h + 1) for h in range(PASSES)]
                 for hs in steps:
                     interleave_h2(hs, rows_before, h2_grouped)
@@ -263,10 +265,16 @@ def tile_randomforestmlp_pa_e_kernel(
                     layer1(e, h, halves, h1_codes, h1_scales, h2_rows)
                 rows_before = h2_rows
             if ready is not None:
-                layer2(e - 2, ready[0], ready[1])
+                if (e - 2) * PASSES < EARLY_GROUPS * SHARE:
+                    layer2(e - 2, ready[0], ready[1])
+                else:
+                    held.append((e - 2, ready[0], ready[1]))
             ready = quantised
             if more:
                 halves, h1_codes, h1_scales = next_halves, next_codes, next_scales
+
+        for tree, codes, scales in held:
+            layer2(tree, codes, scales)
 
         for i in range(ROW_TILES):
             nc.vector.scalar_tensor_tensor(

@@ -21,7 +21,7 @@ PASSES = D_H // K_PASS
 ROW_TILES = BATCH // P
 WORDS = K_PASS // 2
 SHARE = 4
-EARLY_GROUPS = 2
+EARLY_GROUPS = 1
 
 FLOPS = 2 * TREES * BATCH * (D_H * D_K + D_K * D_OUT)
 
@@ -87,14 +87,16 @@ def tile_randomforestmlp_pa_e_kernel(
 
         nc.scalar.dma_start(out=b2_rows[0:TREES, :], in_=b2)
         nc.scalar.dma_start(out=b3_rows[0:TREES, :], in_=b3)
-        def load_w3(s):
-            load_scale_planes(nc, w3_planes[s], w3_scales, s * SHARE)
-            nc.sync.dma_start(
-                out=w3_sb[s][:].bitcast(I32),
-                in_=w3_words[s * SHARE : (s + 1) * SHARE]
-                .rearrange("g p n j -> p g (n j)")
-                .bitcast(I32),
-            )
+        def load_w3(s, pieces):
+            passes = SHARE // pieces
+            for piece in range(pieces):
+                places = slice(piece * passes, (piece + 1) * passes)
+                nc.sync.dma_start(
+                    out=w3_sb[s][:].bitcast(I32)[:, places, :],
+                    in_=w3_words[s * SHARE + places.start : s * SHARE + places.stop]
+                    .rearrange("g p n j -> p g (n j)")
+                    .bitcast(I32),
+                )
 
         for e in range(TREES):
             first_pass = e * PASSES
@@ -110,9 +112,12 @@ def tile_randomforestmlp_pa_e_kernel(
                     .bitcast(I32),
                 )
             if first_pass % SHARE == 0 and 0 < s <= EARLY_GROUPS:
-                load_w3(s - 1)
+                load_scale_planes(nc, w3_planes[s - 1], w3_scales, (s - 1) * SHARE)
+                load_w3(s - 1, 1)
         for s in range(EARLY_GROUPS, groups):
-            load_w3(s)
+            load_scale_planes(nc, w3_planes[s], w3_scales, s * SHARE)
+        for s in range(EARLY_GROUPS, groups):
+            load_w3(s, SHARE if s == groups - 1 else 1)
 
         b2_turned = turns.tile([P, PASSES * PACK, P], BF16, tag="turn", name="b2_turned")
         for h in range(PASSES):

@@ -50,9 +50,13 @@ def tile_randomforestmlp_pa_e_kernel(
 
         h1_sb = [keep.tile([P, ROW_TILES, D_H], BF16, name="h1_sb%d" % e) for e in range(TREES)]
         w2_raw = [
-            [keep.tile([P, PASSES, K_PASS], U32, name="w2_raw%d_%d" % (e, h)) for h in range(PASSES)]
+            [keep.tile([P, PASSES, K_PASS], U32, name="w2_raw%d_%d" % (e, x)) for x in range(PASSES)]
             for e in range(TREES)
         ]
+
+        def by_halves(e):
+            return e in (0, TREES - 1)
+
         w3_sb = [
             keep.tile([P, SHARE, D_OUT], U32, name="w3_sb%d" % s, align_bytes=64)
             for s in range(groups)
@@ -104,13 +108,19 @@ def tile_randomforestmlp_pa_e_kernel(
             nc.sync.dma_start(out=h1_sb[e][:], in_=h1[e].rearrange("(p i) k -> p i k", i=ROW_TILES))
             if first_pass % SHARE == 0:
                 load_scale_planes(nc, w2_planes_raw[s], w2_scales, first_pass)
-            for h in range(PASSES):
-                nc.sync.dma_start(
-                    out=w2_raw[e][h][:].bitcast(I32),
-                    in_=w2_words[first_pass : first_pass + PASSES, :, h * K_PASS : (h + 1) * K_PASS, :]
-                    .rearrange("g p n j -> p g (n j)")
-                    .bitcast(I32),
-                )
+            for x in range(PASSES):
+                if by_halves(e):
+                    nc.sync.dma_start(
+                        out=w2_raw[e][x][:].bitcast(I32),
+                        in_=w2_words[first_pass : first_pass + PASSES, :, x * K_PASS : (x + 1) * K_PASS, :]
+                        .rearrange("g p n j -> p g (n j)")
+                        .bitcast(I32),
+                    )
+                else:
+                    nc.sync.dma_start(
+                        out=w2_raw[e][x][:].rearrange("p h n -> p (h n)").bitcast(I32),
+                        in_=w2_words[first_pass + x].rearrange("p n j -> p (n j)").bitcast(I32),
+                    )
             if first_pass % SHARE == 0 and 0 < s <= EARLY_GROUPS:
                 load_scale_planes(nc, w3_planes[s - 1], w3_scales, (s - 1) * SHARE)
                 load_w3(s - 1, 1)
@@ -167,7 +177,7 @@ def tile_randomforestmlp_pa_e_kernel(
                 in_=w2_planes_raw[s][:].rearrange("p (h m j) -> p h m j", h=PASSES, j=PACK),
             )
 
-        def layer1(e, h, halves, codes, scales, h2_rows):
+        def layer1(e, h, pieces, codes, scales, h2_rows):
             for pair in range(PACK // 2):
                 acc = accs.tile([P, 2, BATCH], F32, tag="acc", name="acc")
                 for v in range(2):
@@ -175,9 +185,10 @@ def tile_randomforestmlp_pa_e_kernel(
                     for g in range(PASSES):
                         s, place = divmod(e * PASSES + g, SHARE)
                         cols = slice(h * K_PASS + j * P, h * K_PASS + (j + 1) * P)
+                        piece, part = (h, g) if by_halves(e) else (g, h)
                         nc.tensor.matmul_mx(
                             out=acc[:, v, :],
-                            lhsT=halves[h][:, g, j, :].bitcast(FP8X4),
+                            lhsT=pieces[piece][:, part, j, :].bitcast(FP8X4),
                             lhsT_scale=w2_planes[s][4 * place : P, cols],
                             rhs=codes[:, g, :].bitcast(FP8X4),
                             rhs_scale=scales[:, g, :],
@@ -225,17 +236,17 @@ def tile_randomforestmlp_pa_e_kernel(
                         stop=(step == last),
                     )
 
-        def sort_half(e, h):
-            half = sorted_pool.tile([P, PASSES, PACK, P], U32, name="w2_sorted%d" % h, align_bytes=64)
+        def sort_piece(e, x):
+            piece = sorted_pool.tile([P, PASSES, PACK, P], U32, name="w2_sorted%d" % x, align_bytes=64)
             nc.vector.tensor_copy(
-                out=half[:].bitcast(I32).rearrange("p g j m -> p g m j"),
-                in_=w2_raw[e][h][:].bitcast(I32).rearrange("p g (m j) -> p g m j", j=PACK),
+                out=piece[:].bitcast(I32).rearrange("p a j m -> p a m j"),
+                in_=w2_raw[e][x][:].bitcast(I32).rearrange("p a (m j) -> p a m j", j=PACK),
             )
-            return half
+            return piece
 
         h1_grouped = turn_h1(0)
         sort_planes(0)
-        halves = [sort_half(0, h) for h in range(PASSES)]
+        pieces = [sort_piece(0, x) for x in range(PASSES)]
         h1_codes, h1_scales = quantise_h1(h1_grouped)
         rows_before = None
         ready = None
@@ -257,7 +268,7 @@ def tile_randomforestmlp_pa_e_kernel(
                 for hs in steps:
                     interleave_h2(hs, rows_before, h2_grouped)
             if more:
-                next_halves = [sort_half(e + 1, h) for h in range(PASSES)]
+                next_pieces = [sort_piece(e + 1, x) for x in range(PASSES)]
                 next_codes, next_scales = quantise_h1(h1_grouped)
             if rows_before is not None:
                 for hs in steps:
@@ -267,7 +278,7 @@ def tile_randomforestmlp_pa_e_kernel(
             if e < TREES:
                 h2_rows = work.tile([P, PASSES, PACK, BATCH], BF16, name="h2_rows")
                 for h in range(PASSES):
-                    layer1(e, h, halves, h1_codes, h1_scales, h2_rows)
+                    layer1(e, h, pieces, h1_codes, h1_scales, h2_rows)
                 rows_before = h2_rows
             if ready is not None:
                 if (e - 2) * PASSES < EARLY_GROUPS * SHARE:
@@ -276,7 +287,7 @@ def tile_randomforestmlp_pa_e_kernel(
                     held.append((e - 2, ready[0], ready[1]))
             ready = quantised
             if more:
-                halves, h1_codes, h1_scales = next_halves, next_codes, next_scales
+                pieces, h1_codes, h1_scales = next_pieces, next_codes, next_scales
 
         for tree, codes, scales in held:
             layer2(tree, codes, scales)

@@ -246,8 +246,9 @@ def tile_randomforestmlp_pa_e_kernel(
 
         h1_grouped = turn_h1(0)
         sort_planes(0)
-        pieces = [sort_piece(0, x) for x in range(PASSES)]
+        pieces = [sort_piece(0, 0)]
         h1_codes, h1_scales = quantise_h1(h1_grouped)
+        pieces.append(sort_piece(0, 1))
         rows_before = None
         ready = None
         held = []
@@ -268,12 +269,15 @@ def tile_randomforestmlp_pa_e_kernel(
                 for hs in steps:
                     interleave_h2(hs, rows_before, h2_grouped)
             if more:
-                next_pieces = [sort_piece(e + 1, x) for x in range(PASSES)]
+                early_pieces = 1 if by_halves(e + 1) else PASSES
+                next_pieces = [sort_piece(e + 1, x) for x in range(early_pieces)]
                 next_codes, next_scales = quantise_h1(h1_grouped)
             if rows_before is not None:
                 for hs in steps:
                     quantise_h2(hs, h2_grouped, h2_codes, h2_scales)
                 quantised = (h2_codes, h2_scales)
+            if more:
+                next_pieces += [sort_piece(e + 1, x) for x in range(early_pieces, PASSES)]
             rows_before = None
             if e < TREES:
                 h2_rows = work.tile([P, PASSES, PACK, BATCH], BF16, name="h2_rows")

@@ -22,6 +22,8 @@ ROW_TILES = BATCH // P
 WORDS = K_PASS // 2
 SHARE = 4
 EARLY_GROUPS = 1
+EARLY_BEHIND = 4
+EARLY_ROUND = 5
 
 FLOPS = 2 * TREES * BATCH * (D_H * D_K + D_K * D_OUT)
 
@@ -121,12 +123,12 @@ def tile_randomforestmlp_pa_e_kernel(
                         out=w2_raw[e][x][:].rearrange("p h n -> p (h n)").bitcast(I32),
                         in_=w2_words[first_pass + x].rearrange("p n j -> p (n j)").bitcast(I32),
                     )
-            if first_pass % SHARE == 0 and 0 < s <= EARLY_GROUPS:
-                load_scale_planes(nc, w3_planes[s - 1], w3_scales, (s - 1) * SHARE)
-                load_w3(s - 1, 1)
+            if e == EARLY_BEHIND:
+                for s in range(EARLY_GROUPS):
+                    load_scale_planes(nc, w3_planes[s], w3_scales, s * SHARE)
+                    load_w3(s, 1)
         for s in range(EARLY_GROUPS, groups):
             load_scale_planes(nc, w3_planes[s], w3_scales, s * SHARE)
-        for s in range(EARLY_GROUPS, groups):
             load_w3(s, SHARE if s == groups - 1 else 1)
 
         b2_turned = turns.tile([P, PASSES * PACK, P], BF16, tag="turn", name="b2_turned")
@@ -285,15 +287,14 @@ def tile_randomforestmlp_pa_e_kernel(
                     layer1(e, h, pieces, h1_codes, h1_scales, h2_rows)
                 rows_before = h2_rows
             if ready is not None:
-                if (e - 2) * PASSES < EARLY_GROUPS * SHARE:
-                    layer2(e - 2, ready[0], ready[1])
-                else:
-                    held.append((e - 2, ready[0], ready[1]))
+                held.append((e - 2, ready[0], ready[1]))
+            if EARLY_ROUND <= e < EARLY_ROUND + EARLY_GROUPS * SHARE // PASSES:
+                layer2(*held[e - EARLY_ROUND])
             ready = quantised
             if more:
                 pieces, h1_codes, h1_scales = next_pieces, next_codes, next_scales
 
-        for tree, codes, scales in held:
+        for tree, codes, scales in held[EARLY_GROUPS * SHARE // PASSES :]:
             layer2(tree, codes, scales)
 
         for i in range(ROW_TILES):

@@ -21,18 +21,20 @@ PASSES = D_H // K_PASS
 ROW_TILES = BATCH // P
 WORDS = K_PASS // 2
 SHARE = 4
+GPSIMD_GROUPS = (1, 2,)
 EARLY_GROUPS = 1
+VECTOR_COLS = 224
 EARLY_BEHIND = 4
 EARLY_ROUND = 5
 
 FLOPS = 2 * TREES * BATCH * (D_H * D_K + D_K * D_OUT)
 
 
-def load_scale_planes(nc, planes, scales, first_pass):
+def load_scale_planes(queue, dtype, planes, scales, first_pass):
     for quad in range(4):
-        nc.sync.dma_start(
-            out=planes[32 * quad : 32 * quad + 4 * SHARE, :].bitcast(I32),
-            in_=scales[first_pass : first_pass + SHARE, 4 * quad : 4 * quad + 4, :].bitcast(I32),
+        queue.dma_start(
+            out=planes[32 * quad : 32 * quad + 4 * SHARE, :].bitcast(dtype),
+            in_=scales[first_pass : first_pass + SHARE, 4 * quad : 4 * quad + 4, :].bitcast(dtype),
         )
 
 
@@ -91,6 +93,8 @@ def tile_randomforestmlp_pa_e_kernel(
         make_identity(nc, ident_bf16[:])
         make_identity(nc, ident_f32[:])
 
+        for s in GPSIMD_GROUPS:
+            load_scale_planes(nc.gpsimd, F32, w2_planes_raw[s], w2_scales, s * SHARE)
         nc.scalar.dma_start(out=b2_rows[0:TREES, :], in_=b2)
         nc.scalar.dma_start(out=b3_rows[0:TREES, :], in_=b3)
         def load_w3(s, pieces):
@@ -108,8 +112,8 @@ def tile_randomforestmlp_pa_e_kernel(
             first_pass = e * PASSES
             s = first_pass // SHARE
             nc.sync.dma_start(out=h1_sb[e][:], in_=h1[e].rearrange("(p i) k -> p i k", i=ROW_TILES))
-            if first_pass % SHARE == 0:
-                load_scale_planes(nc, w2_planes_raw[s], w2_scales, first_pass)
+            if first_pass % SHARE == 0 and s not in GPSIMD_GROUPS:
+                load_scale_planes(nc.sync, I32, w2_planes_raw[s], w2_scales, first_pass)
             for x in range(PASSES):
                 if by_halves(e):
                     nc.sync.dma_start(
@@ -125,10 +129,10 @@ def tile_randomforestmlp_pa_e_kernel(
                     )
             if e == EARLY_BEHIND:
                 for s in range(EARLY_GROUPS):
-                    load_scale_planes(nc, w3_planes[s], w3_scales, s * SHARE)
+                    load_scale_planes(nc.sync, I32, w3_planes[s], w3_scales, s * SHARE)
                     load_w3(s, 1)
         for s in range(EARLY_GROUPS, groups):
-            load_scale_planes(nc, w3_planes[s], w3_scales, s * SHARE)
+            load_scale_planes(nc.sync, I32, w3_planes[s], w3_scales, s * SHARE)
             load_w3(s, SHARE if s == groups - 1 else 1)
 
         b2_turned = turns.tile([P, PASSES * PACK, P], BF16, tag="turn", name="b2_turned")
@@ -206,10 +210,10 @@ def tile_randomforestmlp_pa_e_kernel(
                         bias=b2_cols[:, h * PACK + j, e : e + 1],
                     )
 
-        def interleave_h2(hs, h2_rows, grouped):
-            nc.vector.tensor_copy(
-                out=grouped[:, hs, :].rearrange("p h (c j) -> p h c j", j=PACK),
-                in_=h2_rows[:, hs, :, :].rearrange("p h j c -> p h c j"),
+        def interleave_h2(copy, hs, cs, h2_rows, grouped):
+            copy(
+                out=grouped[:, hs, cs.start * PACK : cs.stop * PACK].rearrange("p h (c j) -> p h c j", j=PACK),
+                in_=h2_rows[:, hs, :, cs].rearrange("p h j c -> p h c j"),
             )
 
         def quantise_h2(hs, grouped, codes, scales):
@@ -268,8 +272,10 @@ def tile_randomforestmlp_pa_e_kernel(
                 h2_codes = keep.tile([P, PASSES, BATCH], U32, name="h2_codes%d" % e, align_bytes=64)
                 h2_scales = keep.tile([P, PASSES, BATCH], U8, name="h2_scales%d" % e, align_bytes=64)
                 steps = [slice(0, PASSES)] if e < TREES else [slice(h, h + 1) for h in range(PASSES)]
+                cut = VECTOR_COLS
                 for hs in steps:
-                    interleave_h2(hs, rows_before, h2_grouped)
+                    interleave_h2(nc.scalar.copy, hs, slice(cut, BATCH), rows_before, h2_grouped)
+                    interleave_h2(nc.vector.tensor_copy, hs, slice(0, cut), rows_before, h2_grouped)
             if more:
                 early_pieces = 1 if by_halves(e + 1) else PASSES
                 next_pieces = [sort_piece(e + 1, x) for x in range(early_pieces)]

from contextlib import ExitStack

import concourse.mybir as mybir
from concourse.masks import make_identity

F32 = mybir.dt.float32
BF16 = mybir.dt.bfloat16
I32 = mybir.dt.int32
U32 = mybir.dt.uint32
U8 = mybir.dt.uint8
FP8X4 = mybir.dt.float8_e4m3fn_x4
ADD = mybir.AluOpType.add
MULT = mybir.AluOpType.mult
RELU = mybir.ActivationFunctionType.Relu

TREES, BATCH, D_H, D_K, D_OUT = 8, 256, 1024, 1024, 256
P = 128
PACK = 4
K_PASS = PACK * P
PASSES = D_H // K_PASS
ROW_TILES = BATCH // P
WORDS = K_PASS // 2
SHARE = 4
GPSIMD_GROUPS = (1, 2,)
EARLY_GROUPS = 1
VECTOR_COLS = 224
EARLY_BEHIND = 4
EARLY_ROUND = 5

FLOPS = 2 * TREES * BATCH * (D_H * D_K + D_K * D_OUT)


def load_scale_planes(queue, dtype, planes, scales, first_pass):
    for quad in range(4):
        queue.dma_start(
            out=planes[32 * quad : 32 * quad + 4 * SHARE, :].bitcast(dtype),
            in_=scales[first_pass : first_pass + SHARE, 4 * quad : 4 * quad + 4, :].bitcast(dtype),
        )


def tile_randomforestmlp_pa_e_kernel(
    tc, h1, w2_words, w2_scales, b2, w3_words, w3_scales, b3, out
):
    nc = tc.nc
    groups = TREES * PASSES // SHARE
    with ExitStack() as ctx:
        ctx.enter_context(tc.manual_schedule())
        keep = ctx.enter_context(tc.tile_pool(name="keep", bufs=1))
        work = ctx.enter_context(tc.tile_pool(name="work", bufs=2))
        sorted_pool = ctx.enter_context(tc.tile_pool(name="sorted", bufs=3))
        outs = ctx.enter_context(tc.psum_pool(name="outs", bufs=1))
        accs = ctx.enter_context(tc.psum_pool(name="accs", bufs=4))
        turns = ctx.enter_context(tc.psum_pool(name="turns", bufs=2))

        h1_sb = [keep.tile([P, ROW_TILES, D_H], BF16, name="h1_sb%d" % e) for e in range(TREES)]
        w2_raw = [
            [keep.tile([P, PASSES, K_PASS], U32, name="w2_raw%d_%d" % (e, x)) for x in range(PASSES)]
            for e in range(TREES)
        ]

        def by_halves(e):
            return e in (0, TREES - 1)

        w3_sb = [
            keep.tile([P, SHARE, D_OUT], U32, name="w3_sb%d" % s, align_bytes=64)
            for s in range(groups)
        ]
        w2_planes_raw = [keep.tile([P, D_K], U8, name="w2_planes_raw%d" % s) for s in range(groups)]
        w2_planes = [
            keep.tile([P, D_K], U8, name="w2_planes%d" % s, align_bytes=64) for s in range(groups)
        ]
        w3_planes = [
            keep.tile([P, D_OUT], U8, name="w3_planes%d" % s, align_bytes=64)
            for s in range(groups)
        ]
        b2_rows = keep.tile([P, D_K], BF16)
        b3_rows = keep.tile([P, D_OUT], BF16)
        eighth = keep.tile([P, P], BF16)
        ident_f32 = keep.tile([P, P], F32)
        ident_bf16 = keep.tile([P, P], BF16)
        b2_cols = keep.tile([P, PASSES * PACK, TREES], F32)
        b3_mean = keep.tile([P, D_OUT], F32)
        out_sb = keep.tile([P, ROW_TILES, D_OUT], F32)

        nc.vector.memset(b2_rows[:], 0.0)
        nc.vector.memset(w2_planes_raw[0][:].bitcast(I32), 0)
        nc.vector.memset(b3_rows[:], 0.0)
        nc.vector.memset(eighth[:], 1.0 / TREES)
        for s in range(groups):
            if s > 0:
                nc.vector.memset(w2_planes_raw[s][:].bitcast(I32), 0)
            nc.vector.memset(w3_planes[s][:].bitcast(I32), 0)
        make_identity(nc, ident_bf16[:])
        make_identity(nc, ident_f32[:])

        for s in GPSIMD_GROUPS:
            load_scale_planes(nc.gpsimd, F32, w2_planes_raw[s], w2_scales, s * SHARE)
        nc.scalar.dma_start(out=b2_rows[0:TREES, :], in_=b2)
        nc.scalar.dma_start(out=b3_rows[0:TREES, :], in_=b3)
        def load_w3(s, pieces):
            passes = SHARE // pieces
            for piece in range(pieces):
                places = slice(piece * passes, (piece + 1) * passes)
                nc.sync.dma_start(
                    out=w3_sb[s][:].bitcast(I32)[:, places, :],
                    in_=w3_words[s * SHARE + places.start : s * SHARE + places.stop]
                    .rearrange("g p n j -> p g (n j)")
                    .bitcast(I32),
                )

        for e in range(TREES):
            first_pass = e * PASSES
            s = first_pass // SHARE
            nc.sync.dma_start(out=h1_sb[e][:], in_=h1[e].rearrange("(p i) k -> p i k", i=ROW_TILES))
            if first_pass % SHARE == 0 and s not in GPSIMD_GROUPS:
                load_scale_planes(nc.sync, I32, w2_planes_raw[s], w2_scales, first_pass)
            for x in range(PASSES):
                if by_halves(e):
                    nc.sync.dma_start(
                        out=w2_raw[e][x][:].bitcast(I32),
                        in_=w2_words[first_pass : first_pass + PASSES, :, x * K_PASS : (x + 1) * K_PASS, :]
                        .rearrange("g p n j -> p g (n j)")
                        .bitcast(I32),
                    )
                else:
                    nc.sync.dma_start(
                        out=w2_raw[e][x][:].rearrange("p h n -> p (h n)").bitcast(I32),
                        in_=w2_words[first_pass + x].rearrange("p n j -> p (n j)").bitcast(I32),
                    )
            if e == EARLY_BEHIND:
                for s in range(EARLY_GROUPS):
                    load_scale_planes(nc.sync, I32, w3_planes[s], w3_scales, s * SHARE)
                    load_w3(s, 1)
        for s in range(EARLY_GROUPS, groups):
            load_scale_planes(nc.sync, I32, w3_planes[s], w3_scales, s * SHARE)
            load_w3(s, SHARE if s == groups - 1 else 1)

        b2_turned = turns.tile([P, PASSES * PACK, P], BF16, tag="turn", name="b2_turned")
        for h in range(PASSES):
            for j in range(PACK):
                nc.tensor.transpose(
                    b2_turned[:, h * PACK + j, :],
                    b2_rows[:, h * K_PASS + j : (h + 1) * K_PASS : PACK],
                    ident_bf16[:],
                )
        nc.scalar.copy(out=b2_cols[:], in_=b2_turned[:, :, 0:TREES])

        mean_ps = turns.tile([P, D_OUT], F32, tag="turn", name="mean_ps")
        nc.tensor.matmul(mean_ps[:], lhsT=eighth[:], rhs=b3_rows[:], start=True, stop=True)
        nc.scalar.copy(out=b3_mean[:], in_=mean_ps[:])

        def turn_h1(e):
            h1_words = h1_sb[e][:].bitcast(F32)
            grouped = work.tile([P, PASSES, PACK * BATCH], BF16, name="h1_grouped", align_bytes=64)
            for g in range(PASSES):
                turned = turns.tile([P, 2, BATCH], F32, tag="turn", name="turned")
                for u in range(2):
                    for i in range(ROW_TILES):
                        nc.tensor.transpose(
                            turned[:, u, i * P : (i + 1) * P],
                            h1_words[:, i, g * WORDS + u : (g + 1) * WORDS : 2],
                            ident_f32[:],
                        )
                nc.scalar.copy(
                    out=grouped[:, g, :].bitcast(F32).rearrange("p (c u) -> p c u", u=2),
                    in_=turned[:].rearrange("p u c -> p c u"),
                )
            return grouped

        def quantise_h1(grouped):
            codes = work.tile([P, PASSES, BATCH], U32, name="h1_codes", align_bytes=64)
            scales = work.tile([P, PASSES, BATCH], U8, name="h1_scales", align_bytes=64)
            nc.vector.quantize_mx(
                out=codes[:].rearrange("p g c -> p (g c)").bitcast(FP8X4),
                scales=scales[:].rearrange("p g c -> p (g c)"),
                in_=grouped[:].rearrange("p g x -> p (g x)"),
            )
            return codes, scales

        def sort_planes(s):
            nc.vector.tensor_copy(
                out=w2_planes[s][:].rearrange("p (h j m) -> p h m j", h=PASSES, j=PACK),
                in_=w2_planes_raw[s][:].rearrange("p (h m j) -> p h m j", h=PASSES, j=PACK),
            )

        def layer1(e, h, pieces, codes, scales, h2_rows):
            for pair in range(PACK // 2):
                acc = accs.tile([P, 2, BATCH], F32, tag="acc", name="acc")
                for v in range(2):
                    j = 2 * pair + v
                    for g in range(PASSES):
                        s, place = divmod(e * PASSES + g, SHARE)
                        cols = slice(h * K_PASS + j * P, h * K_PASS + (j + 1) * P)
                        piece, part = (h, g) if by_halves(e) else (g, h)
                        nc.tensor.matmul_mx(
                            out=acc[:, v, :],
                            lhsT=pieces[piece][:, part, j, :].bitcast(FP8X4),
                            lhsT_scale=w2_planes[s][4 * place : P, cols],
                            rhs=codes[:, g, :].bitcast(FP8X4),
                            rhs_scale=scales[:, g, :],
                            start=(g == 0),
                            stop=(g == PASSES - 1),
                        )
                for v in range(2):
                    j = 2 * pair + v
                    nc.scalar.activation(
                        out=h2_rows[:, h, j, :],
                        in_=acc[:, v, :],
                        func=RELU,
                        bias=b2_cols[:, h * PACK + j, e : e + 1],
                    )

        def interleave_h2(copy, hs, cs, h2_rows, grouped):
            copy(
                out=grouped[:, hs, cs.start * PACK : cs.stop * PACK].rearrange("p h (c j) -> p h c j", j=PACK),
                in_=h2_rows[:, hs, :, cs].rearrange("p h j c -> p h c j"),
            )

        def quantise_h2(hs, grouped, codes, scales):
            nc.vector.quantize_mx(
                out=codes[:, hs, :].rearrange("p h c -> p (h c)").bitcast(FP8X4),
                scales=scales[:, hs, :].rearrange("p h c -> p (h c)"),
                in_=grouped[:, hs, :].rearrange("p h x -> p (h x)"),
            )

        out_acc = [outs.tile([P, D_OUT], F32, name="out_acc%d" % i) for i in range(ROW_TILES)]
        last = TREES * PASSES - 1

        def layer2(e, codes, scales):
            for h in range(PASSES):
                step = e * PASSES + h
                s, place = divmod(step, SHARE)
                for i in range(ROW_TILES):
                    rows = slice(i * P, (i + 1) * P)
                    nc.tensor.matmul_mx(
                        out=out_acc[i][:],
                        lhsT=codes[:, h, rows].bitcast(FP8X4),
                        lhsT_scale=scales[:, h, rows],
                        rhs=w3_sb[s][:, place, :].bitcast(FP8X4),
                        rhs_scale=w3_planes[s][4 * place : P, :],
                        start=(step == 0),
                        stop=(step == last),
                    )

        def sort_piece(e, x):
            piece = sorted_pool.tile([P, PASSES, PACK, P], U32, name="w2_sorted%d" % x, align_bytes=64)
            nc.vector.tensor_copy(
                out=piece[:].bitcast(I32).rearrange("p a j m -> p a m j"),
                in_=w2_raw[e][x][:].bitcast(I32).rearrange("p a (m j) -> p a m j", j=PACK),
            )
            return piece

        h1_grouped = turn_h1(0)
        sort_planes(0)
        pieces = [sort_piece(0, 0)]
        h1_codes, h1_scales = quantise_h1(h1_grouped)
        pieces.append(sort_piece(0, 1))
        rows_before = None
        ready = None
        held = []
        for e in range(TREES + 2):
            more = e + 1 < TREES
            quantised = None
            if more:
                h1_grouped = turn_h1(e + 1)
                if (e + 1) * PASSES % SHARE == 0:
                    sort_planes((e + 1) * PASSES // SHARE)
            if rows_before is not None:
                h2_grouped = work.tile(
                    [P, PASSES, PACK * BATCH], BF16, name="h2_grouped", align_bytes=64
                )
                h2_codes = keep.tile([P, PASSES, BATCH], U32, name="h2_codes%d" % e, align_bytes=64)
                h2_scales = keep.tile([P, PASSES, BATCH], U8, name="h2_scales%d" % e, align_bytes=64)
                steps = [slice(0, PASSES)] if e < TREES else [slice(h, h + 1) for h in range(PASSES)]
                cut = VECTOR_COLS
                for hs in steps:
                    interleave_h2(nc.scalar.copy, hs, slice(cut, BATCH), rows_before, h2_grouped)
                    interleave_h2(nc.vector.tensor_copy, hs, slice(0, cut), rows_before, h2_grouped)
            if more:
                early_pieces = 1 if by_halves(e + 1) else PASSES
                next_pieces = [sort_piece(e + 1, x) for x in range(early_pieces)]
                next_codes, next_scales = quantise_h1(h1_grouped)
            if rows_before is not None:
                for hs in steps:
                    quantise_h2(hs, h2_grouped, h2_codes, h2_scales)
                quantised = (h2_codes, h2_scales)
            if more:
                next_pieces += [sort_piece(e + 1, x) for x in range(early_pieces, PASSES)]
            rows_before = None
            if e < TREES:
                h2_rows = work.tile([P, PASSES, PACK, BATCH], BF16, name="h2_rows")
                for h in range(PASSES):
                    layer1(e, h, pieces, h1_codes, h1_scales, h2_rows)
                rows_before = h2_rows
            if ready is not None:
                held.append((e - 2, ready[0], ready[1]))
            if EARLY_ROUND <= e < EARLY_ROUND + EARLY_GROUPS * SHARE // PASSES:
                layer2(*held[e - EARLY_ROUND])
            ready = quantised
            if more:
                pieces, h1_codes, h1_scales = next_pieces, next_codes, next_scales

        for tree, codes, scales in held[EARLY_GROUPS * SHARE // PASSES :]:
            layer2(tree, codes, scales)

        for i in range(ROW_TILES):
            nc.vector.scalar_tensor_tensor(
                out=out_sb[:, i, :],
                in0=out_acc[i][:],
                scalar=1.0 / TREES,
                in1=b3_mean[:],
                op0=MULT,
                op1=ADD,
            )
        nc.sync.dma_start(out=out.rearrange("(p i) d -> p i d", i=ROW_TILES), in_=out_sb[:])
